import numpy as np
import ml_dtypes


def mxq(x, axis, fmt="e4m3"):
    dtype, down = {"e4m3": (ml_dtypes.float8_e4m3fn, 7), "e5m2": (ml_dtypes.float8_e5m2, 14)}[fmt]
    v = np.moveaxis(np.asarray(x, np.float32).astype(ml_dtypes.bfloat16).astype(np.float64), axis, -1)
    blocks = v.reshape(v.shape[:-1] + (-1, 32))
    amax = np.abs(blocks).max(-1, keepdims=True)
    byte = np.maximum(np.where(amax > 0, np.frexp(amax)[1] - 1 + 127, 0) - down, 1)
    scale = np.exp2(byte - 127.0)
    codes = (blocks / scale).astype(np.float32).astype(dtype).astype(np.float64)
    return np.moveaxis((codes * scale).reshape(v.shape), -1, axis)


WIDE = False


def mx_kscale(k):
    if not WIDE:
        return np.ones(k)
    levels = np.array([10, -10, 5, -5, 0])
    a = np.random.permutation(np.resize(levels, k // 512 * 4)).reshape(k // 512, 4)
    idx = np.arange(k)
    return np.exp2(a[idx // 512, idx % 128 // 32])


BF16 = ml_dtypes.bfloat16


def bf(x):
    return np.asarray(x, np.float32).astype(BF16)


def f64(x):
    return np.asarray(x).astype(np.float64)


B, I, O, K = 4096, 256, 128, 16
C = I * K
X_ABS_MAX = 2.8


def photonic_basis(u, b_coef):
    u3 = u[:, :, None]
    b1, b2, b3, b4, b5, b6, b7, b8 = (b_coef[:, j] for j in range(8))
    inner_base = np.expm1(b3 * u3)
    powered = np.power(inner_base, b4)
    inner_log = np.log1p(powered)
    outer = 1.0 + b2 * inner_log
    return b1 * np.log(outer) + b5 * u3 + b6 * u3**2 + b7 * u3**3 + b8 * u3**4


def setup_inputs():
    kk = np.arange(K)
    t = mx_kscale(C).reshape(K, I)[kk, (32 * kk) % I]
    x = (np.random.uniform(size=(B, I)) * 2.0 - 1.0) * X_ABS_MAX
    coeffs = np.random.standard_normal((O, I, K)) * 1.5 / np.sqrt(C) / t
    b1 = np.random.uniform(0.5, 1.5, K) * t
    b2 = np.random.uniform(0.5, 1.5, K)
    b3 = np.random.uniform(0.01, 0.03, K)
    b4 = np.random.uniform(1.0, 3.0, K)
    b5 = np.random.uniform(-1.0, 1.0, K) * 1e-2 * t
    b6 = np.random.uniform(-1.0, 1.0, K) * 2e-4 * t
    b7 = np.random.uniform(-1.0, 1.0, K) * 4e-6 * t
    b8 = np.random.uniform(-1.0, 1.0, K) * 8e-8 * t
    b_coef = np.stack([b1, b2, b3, b4, b5, b6, b7, b8], axis=1)
    alpha = np.random.uniform(8.0, 10.0, I)
    beta = np.random.uniform(29.0, 31.0, I)
    return {"x": bf(x), "coeffs": bf(coeffs), "b_coef": bf(b_coef), "alpha": bf(alpha), "beta": bf(beta)}


def reference(x, coeffs, b_coef, alpha, beta):
    u = f64(alpha)[None, :] * f64(x) + f64(beta)[None, :]
    basis = photonic_basis(u, f64(b_coef))
    bk = basis.transpose(0, 2, 1).reshape(B, C)
    ck = f64(coeffs).transpose(0, 2, 1).reshape(O, C)
    return mxq(bk, 1, "e4m3") @ mxq(ck, 1, "e4m3").T

@@ -1,0 +1,234 @@
+from contextlib import ExitStack
+
+import concourse.mybir as mybir
+from concourse.masks import make_identity
+
+F32 = mybir.dt.float32
+BF16 = mybir.dt.bfloat16
+U32 = mybir.dt.uint32
+U8 = mybir.dt.uint8
+FP8X4 = mybir.dt.float8_e4m3fn_x4
+ACT = mybir.ActivationFunctionType
+ALU = mybir.AluOpType
+
+B, I, O, K = 4096, 256, 128, 16
+P = 128
+PACK = 4
+HALF = P // 2
+PASSES = K // 2
+SUB = 4
+CHUNK = SUB * P
+CHUNKS = B // CHUNK
+COLS = CHUNK * PACK
+RING = 4
+B1, B2, B3, B4, B5, B6, B7, B8 = range(8)
+
+FLOPS = 2 * B * I * K * O
+
+
+def tile_photonicbasisactivationlayerintervalaffi_kernel(tc, x, coeffs, b_coef, alpha, beta, out):
+    nc = tc.nc
+    x_rows = x.rearrange("(c p s) i -> c p s i", p=P, s=SUB)
+    out_rows = out.rearrange("(c p s) o -> c p s o", p=P, s=SUB)
+
+    with ExitStack() as ctx:
+        keep = ctx.enter_context(tc.tile_pool(name="keep", bufs=1))
+        x_pool = ctx.enter_context(tc.tile_pool(name="x_pool", bufs=2))
+        u_pool = ctx.enter_context(tc.tile_pool(name="u_pool", bufs=2))
+        basis_pool = ctx.enter_context(tc.tile_pool(name="basis_pool", bufs=3))
+        res_pool = ctx.enter_context(tc.tile_pool(name="res_pool", bufs=2))
+        ring = ctx.enter_context(tc.tile_pool(name="ring", bufs=RING))
+        psum_x = ctx.enter_context(tc.psum_pool(name="psum_x", bufs=2))
+        psum_acc = ctx.enter_context(tc.psum_pool(name="psum_acc", bufs=2))
+        ctx.enter_context(tc.manual_schedule())
+
+        ident = keep.tile([P, P], BF16, name="ident")
+        b_all = keep.tile([P, K * 8], BF16, name="b_all")
+        par = keep.tile([P, PASSES, 8], F32, name="par")
+        alpha_bf = keep.tile([P, PACK], BF16, name="alpha_bf")
+        beta_bf = keep.tile([P, PACK], BF16, name="beta_bf")
+        affine = keep.tile([P, 2, PACK], F32, name="affine")
+        neg = keep.tile([P, PASSES, 8], F32, name="neg")
+        halved = keep.tile([P, PASSES, 8], F32, name="halved")
+        ones = keep.tile([P, 1], F32, name="ones")
+        w_codes = keep.tile([P, PASSES, O], U32, name="w_codes", align_bytes=64)
+        w_scales = keep.tile([P, PASSES, O], U8, name="w_scales", align_bytes=64)
+        chain = [keep.tile([P, COLS], F32, name="chain%d" % g) for g in range(PASSES)]
+        poly = [keep.tile([P, COLS], F32, name="poly%d" % g) for g in range(PASSES)]
+        codes = keep.tile([P, PASSES, CHUNK], U32, name="codes", align_bytes=64)
+        scales = keep.tile([P, PASSES, CHUNK], U8, name="scales", align_bytes=64)
+
+        def coef(g, j):
+            return par[:, g, j : j + 1]
+
+        def load_x(c):
+            x_twice = x_pool.tile([P, SUB, 2 * I], BF16, name="x_twice")
+            for h in range(2):
+                nc.sync.dma_start(out=x_twice[:, :, h * I : (h + 1) * I], in_=x_rows[c])
+            return x_twice
+
+        def make_u(x_twice):
+            u = u_pool.tile([P, SUB, P, PACK], F32, name="u")
+            for pair in range(SUB // 2):
+                x_t = psum_x.tile([P, 2, PACK, P], BF16, name="x_t")
+                for s in range(2):
+                    columns = x_twice[:, 2 * pair + s, :].rearrange("p (m t) -> p t m", t=PACK)
+                    for t in range(PACK):
+                        nc.tensor.transpose(x_t[:, s, t, :], columns[:, t, :], ident[:])
+                nc.vector.tensor_tensor(
+                    out=u[:, 2 * pair : 2 * pair + 2, :, :],
+                    in0=x_t[:].rearrange("p s t b -> p s b t"),
+                    in1=affine[:, 0:1, :].unsqueeze(1).to_broadcast([P, 2, P, PACK]),
+                    op=ALU.mult,
+                )
+            nc.vector.tensor_tensor(
+                out=u[:],
+                in0=u[:],
+                in1=affine[:, 1:2, :].unsqueeze(1).to_broadcast([P, SUB, P, PACK]),
+                op=ALU.add,
+            )
+            return u[:].rearrange("p s b t -> p (s b t)")
+
+        def load_coeffs():
+            w_runs = coeffs.rearrange("o (q t) k -> q o (t k)", t=PACK)
+            w_raw = []
+            for part in range(2):
+                o_part = slice(part * O // 2, (part + 1) * O // 2)
+                raw = ring.tile([P, O // 2, PACK * K], BF16, name="w_raw", tag="ring", align_bytes=64)
+                nc.sync.dma_start(out=raw[0:HALF, :, :], in_=w_runs[:, o_part, :])
+                nc.sync.dma_start(out=raw[HALF:P, :, 0 : PACK * K - 1], in_=w_runs[:, o_part, 1 : PACK * K])
+                w_raw.append(raw)
+            return w_raw
+
+        def quantise_coeffs(w_raw):
+            w_grouped = ring.tile([P, PASSES, O, PACK], BF16, name="w_grouped", tag="ring", align_bytes=64)
+            for part in range(2):
+                nc.vector.tensor_copy(
+                    out=w_grouped[:, :, part * O // 2 : (part + 1) * O // 2, :],
+                    in_=w_raw[part][:].rearrange("p o (t g h) -> p g o t h", t=PACK, h=2)[:, :, :, :, 0],
+                )
+            nc.vector.quantize_mx(
+                out=w_codes[:].rearrange("p g o -> p (g o)").bitcast(FP8X4),
+                scales=w_scales[:].rearrange("p g o -> p (g o)"),
+                in_=w_grouped[:].rearrange("p g o t -> p (g o t)"),
+            )
+
+        def tanh_stage(u):
+            for g in range(PASSES):
+                nc.scalar.activation(out=chain[g][:], in_=u, func=ACT.Tanh, scale=halved[:, g, B3 : B3 + 1])
+
+        def polynomial_start(u):
+            for g in range(PASSES):
+                nc.vector.tensor_scalar(
+                    out=poly[g][:], in0=u, scalar1=coef(g, B8), scalar2=coef(g, B7), op0=ALU.mult, op1=ALU.add
+                )
+
+        def polynomial_times_u(u):
+            for g in range(PASSES):
+                nc.vector.tensor_tensor(out=poly[g][:], in0=poly[g][:], in1=u, op=ALU.mult)
+
+        def polynomial_step(u, g, j):
+            nc.vector.scalar_tensor_tensor(
+                out=poly[g][:], in0=poly[g][:], scalar=coef(g, j), in1=u, op0=ALU.add, op1=ALU.mult
+            )
+
+        def log_expm1_stage(u):
+            for g in range(PASSES):
+                log_2t = ring.tile([P, COLS], F32, name="log_2t", tag="ring", align_bytes=64)
+                nc.scalar.activation(out=log_2t[:], in_=chain[g][:], func=ACT.Ln, scale=2.0)
+                nc.scalar.activation(out=chain[g][:], in_=chain[g][:], func=ACT.Ln, scale=-1.0, bias=ones[:, 0:1])
+                nc.vector.tensor_tensor(out=chain[g][:], in0=log_2t[:], in1=chain[g][:], op=ALU.subtract)
+                polynomial_step(u, g, B6)
+
+        def log1p_pow_stage():
+            for g in range(PASSES):
+                nc.scalar.activation(out=chain[g][:], in_=chain[g][:], func=ACT.Sigmoid, scale=neg[:, g, B4 : B4 + 1])
+            for g in range(PASSES):
+                nc.scalar.activation(out=chain[g][:], in_=chain[g][:], func=ACT.Ln)
+
+        def last_log():
+            for g in range(PASSES):
+                nc.scalar.activation(
+                    out=chain[g][:], in_=chain[g][:], func=ACT.Ln, scale=neg[:, g, B2 : B2 + 1], bias=ones[:, 0:1]
+                )
+
+        def quantise_basis():
+            waiting = []
+            for g in range(PASSES + 1):
+                if g < PASSES:
+                    basis = basis_pool.tile([P, COLS], BF16, name="basis", align_bytes=64)
+                    nc.vector.scalar_tensor_tensor(
+                        out=basis[:], in0=chain[g][:], scalar=coef(g, B1), in1=poly[g][:], op0=ALU.mult, op1=ALU.add
+                    )
+                    waiting.append(basis)
+                if g > 0:
+                    nc.vector.quantize_mx(
+                        out=codes[:, g - 1, :].bitcast(FP8X4), scales=scales[:, g - 1, :], in_=waiting[g - 1][:]
+                    )
+
+        def multiply():
+            acc = psum_acc.tile([P, SUB, O], F32, name="acc")
+            for s in range(SUB):
+                rows = slice(s * P, (s + 1) * P)
+                for g in range(PASSES):
+                    nc.tensor.matmul_mx(
+                        out=acc[:, s, :],
+                        lhsT=codes[:, g, rows].bitcast(FP8X4),
+                        lhsT_scale=scales[:, g, rows],
+                        rhs=w_codes[:, g, :].bitcast(FP8X4),
+                        rhs_scale=w_scales[:, g, :],
+                        start=(g == 0),
+                        stop=(g == PASSES - 1),
+                    )
+            return acc
+
+        def store(c, acc):
+            res = res_pool.tile([P, SUB, O], F32, name="res")
+            nc.vector.tensor_copy(out=res[:], in_=acc[:])
+            nc.sync.dma_start(out=out_rows[c], in_=res[:])
+
+        x_next = load_x(0)
+        make_identity(nc, ident[:])
+        i_on_partitions = "(q t) -> q t"
+        for h in range(2):
+            half = slice(h * HALF, (h + 1) * HALF)
+            nc.scalar.dma_start(out=alpha_bf[half, :], in_=alpha.rearrange(i_on_partitions, t=PACK))
+            nc.scalar.dma_start(out=beta_bf[half, :], in_=beta.rearrange(i_on_partitions, t=PACK))
+        nc.scalar.dma_start(out=b_all[:], in_=b_coef.rearrange("k j -> (k j)").partition_broadcast(P))
+        nc.vector.memset(ones[:], 1.0)
+        nc.vector.tensor_copy(out=affine[:, 0, :], in_=alpha_bf[:])
+        nc.vector.tensor_copy(out=affine[:, 1, :], in_=beta_bf[:])
+        for h in range(2):
+            half = slice(h * HALF, (h + 1) * HALF)
+            nc.vector.tensor_copy(
+                out=par[half, :, :],
+                in_=b_all[half, :].rearrange("p (g h j) -> p g h j", h=2, j=8)[:, :, h, :],
+            )
+        nc.vector.tensor_scalar(out=neg[:], in0=par[:], scalar1=-1.0, scalar2=None, op0=ALU.mult)
+        nc.vector.tensor_scalar(out=halved[:], in0=par[:], scalar1=0.5, scalar2=None, op0=ALU.mult)
+        u_next = make_u(x_next)
+        x_next = load_x(1)
+        w_raw = load_coeffs()
+
+        acc = None
+        for c in range(CHUNKS):
+            u = u_next
+            tanh_stage(u)
+            polynomial_start(u)
+            if c == 0:
+                quantise_coeffs(w_raw)
+            polynomial_times_u(u)
+            log_expm1_stage(u)
+            log1p_pow_stage()
+            for g in range(PASSES):
+                polynomial_step(u, g, B5)
+            if c > 0:
+                store(c - 1, acc)
+            if c + 1 < CHUNKS:
+                u_next = make_u(x_next)
+            if c + 2 < CHUNKS:
+                x_next = load_x(c + 2)
+            last_log()
+            quantise_basis()
+            acc = multiply()
+        store(CHUNKS - 1, acc)

@@ -1,3 +1,4 @@
+import math
 from contextlib import ExitStack
 
 import concourse.mybir as mybir
@@ -21,6 +22,7 @@ CHUNK = SUB * P
 CHUNKS = B // CHUNK
 COLS = CHUNK * PACK
 RING = 4
+SHIFT = 32.0
 B1, B2, B3, B4, B5, B6, B7, B8 = range(8)
 
 FLOPS = 2 * B * I * K * O
@@ -51,6 +53,8 @@ def tile_photonicbasisactivationlayerintervalaffi_kernel(tc, x, coeffs, b_coef, 
         neg = keep.tile([P, PASSES, 8], F32, name="neg")
         halved = keep.tile([P, PASSES, 8], F32, name="halved")
         ones = keep.tile([P, 1], F32, name="ones")
+        minus_ones = keep.tile([P, 1], F32, name="minus_ones")
+        shift = keep.tile([P, 1], F32, name="shift")
         w_codes = keep.tile([P, PASSES, O], U32, name="w_codes", align_bytes=64)
         w_scales = keep.tile([P, PASSES, O], U8, name="w_scales", align_bytes=64)
         chain = [keep.tile([P, COLS], F32, name="chain%d" % g) for g in range(PASSES)]
@@ -115,7 +119,7 @@ def tile_photonicbasisactivationlayerintervalaffi_kernel(tc, x, coeffs, b_coef, 
 
         def tanh_stage(u):
             for g in range(PASSES):
-                nc.scalar.activation(out=chain[g][:], in_=u, func=ACT.Tanh, scale=halved[:, g, B3 : B3 + 1])
+                nc.scalar.activation(out=chain[g][:], in_=u, func=ACT.Sigmoid, scale=par[:, g, B3 : B3 + 1], bias=shift[:, 0:1])
 
         def polynomial_start(u):
             for g in range(PASSES):
@@ -134,10 +138,7 @@ def tile_photonicbasisactivationlayerintervalaffi_kernel(tc, x, coeffs, b_coef, 
 
         def log_expm1_stage(u):
             for g in range(PASSES):
-                log_2t = ring.tile([P, COLS], F32, name="log_2t", tag="ring", align_bytes=64)
-                nc.scalar.activation(out=log_2t[:], in_=chain[g][:], func=ACT.Ln, scale=2.0)
-                nc.scalar.activation(out=chain[g][:], in_=chain[g][:], func=ACT.Ln, scale=-1.0, bias=ones[:, 0:1])
-                nc.vector.tensor_tensor(out=chain[g][:], in0=log_2t[:], in1=chain[g][:], op=ALU.subtract)
+                nc.scalar.activation(out=chain[g][:], in_=chain[g][:], func=ACT.Ln, scale=math.exp(SHIFT), bias=minus_ones[:, 0:1])
                 polynomial_step(u, g, B6)
 
         def log1p_pow_stage():
@@ -196,6 +197,8 @@ def tile_photonicbasisactivationlayerintervalaffi_kernel(tc, x, coeffs, b_coef, 
             nc.scalar.dma_start(out=beta_bf[half, :], in_=beta.rearrange(i_on_partitions, t=PACK))
         nc.scalar.dma_start(out=b_all[:], in_=b_coef.rearrange("k j -> (k j)").partition_broadcast(P))
         nc.vector.memset(ones[:], 1.0)
+        nc.vector.memset(minus_ones[:], -1.0)
+        nc.vector.memset(shift[:], -SHIFT)
         nc.vector.tensor_copy(out=affine[:, 0, :], in_=alpha_bf[:])
         nc.vector.tensor_copy(out=affine[:, 1, :], in_=beta_bf[:])
         for h in range(2):

@@ -21,7 +21,12 @@ SUB = 4
 CHUNK = SUB * P
 CHUNKS = B // CHUNK
 COLS = CHUNK * PACK
-RING = 4
+TILES = CHUNKS * PASSES
+BANK = 512
+BATCH = 7
+AHEAD = 9
+W_PARTS = 4
+W_PART = O // W_PARTS
 SHIFT = 32.0
 B1, B2, B3, B4, B5, B6, B7, B8 = range(8)
 
@@ -35,35 +40,29 @@ def tile_photonicbasisactivationlayerintervalaffi_kernel(tc, x, coeffs, b_coef, 
 
     with ExitStack() as ctx:
         keep = ctx.enter_context(tc.tile_pool(name="keep", bufs=1))
-        x_pool = ctx.enter_context(tc.tile_pool(name="x_pool", bufs=2))
-        u_pool = ctx.enter_context(tc.tile_pool(name="u_pool", bufs=2))
-        basis_pool = ctx.enter_context(tc.tile_pool(name="basis_pool", bufs=3))
-        res_pool = ctx.enter_context(tc.tile_pool(name="res_pool", bufs=2))
-        ring = ctx.enter_context(tc.tile_pool(name="ring", bufs=RING))
+        x_pool = ctx.enter_context(tc.tile_pool(name="x_pool", bufs=1))
+        u_pool = ctx.enter_context(tc.tile_pool(name="u_pool", bufs=3))
+        chain_pool = ctx.enter_context(tc.tile_pool(name="chain_pool", bufs=2 * BATCH))
+        poly_pool = ctx.enter_context(tc.tile_pool(name="poly_pool", bufs=AHEAD))
+        basis_pool = ctx.enter_context(tc.tile_pool(name="basis_pool", bufs=2))
+        codes_pool = ctx.enter_context(tc.tile_pool(name="codes_pool", bufs=2))
+        res_pool = ctx.enter_context(tc.tile_pool(name="res_pool", bufs=1))
         psum_x = ctx.enter_context(tc.psum_pool(name="psum_x", bufs=2))
-        psum_acc = ctx.enter_context(tc.psum_pool(name="psum_acc", bufs=2))
+        psum_acc = ctx.enter_context(tc.psum_pool(name="psum_acc", bufs=1))
         ctx.enter_context(tc.manual_schedule())
 
         ident = keep.tile([P, P], BF16, name="ident")
         b_all = keep.tile([P, K * 8], BF16, name="b_all")
         par = keep.tile([P, PASSES, 8], F32, name="par")
+        neg = keep.tile([P, PASSES, 8], F32, name="neg")
         alpha_bf = keep.tile([P, PACK], BF16, name="alpha_bf")
         beta_bf = keep.tile([P, PACK], BF16, name="beta_bf")
         affine = keep.tile([P, 2, PACK], F32, name="affine")
-        neg = keep.tile([P, PASSES, 8], F32, name="neg")
-        halved = keep.tile([P, PASSES, 8], F32, name="halved")
         ones = keep.tile([P, 1], F32, name="ones")
         minus_ones = keep.tile([P, 1], F32, name="minus_ones")
-        shift = keep.tile([P, 1], F32, name="shift")
+        minus_shift = keep.tile([P, 1], F32, name="minus_shift")
         w_codes = keep.tile([P, PASSES, O], U32, name="w_codes", align_bytes=64)
         w_scales = keep.tile([P, PASSES, O], U8, name="w_scales", align_bytes=64)
-        chain = [keep.tile([P, COLS], F32, name="chain%d" % g) for g in range(PASSES)]
-        poly = [keep.tile([P, COLS], F32, name="poly%d" % g) for g in range(PASSES)]
-        codes = keep.tile([P, PASSES, CHUNK], U32, name="codes", align_bytes=64)
-        scales = keep.tile([P, PASSES, CHUNK], U8, name="scales", align_bytes=64)
-
-        def coef(g, j):
-            return par[:, g, j : j + 1]
 
         def load_x(c):
             x_twice = x_pool.tile([P, SUB, 2 * I], BF16, name="x_twice")
@@ -72,7 +71,7 @@ def tile_photonicbasisactivationlayerintervalaffi_kernel(tc, x, coeffs, b_coef, 
             return x_twice
 
         def make_u(x_twice):
-            u = u_pool.tile([P, SUB, P, PACK], F32, name="u")
+            u = u_pool.tile([P, SUB, P, PACK], F32, name="u", tag="u", align_bytes=64)
             for pair in range(SUB // 2):
                 x_t = psum_x.tile([P, 2, PACK, P], BF16, name="x_t")
                 for s in range(2):
@@ -93,102 +92,154 @@ def tile_photonicbasisactivationlayerintervalaffi_kernel(tc, x, coeffs, b_coef, 
             )
             return u[:].rearrange("p s b t -> p (s b t)")
 
-        def load_coeffs():
-            w_runs = coeffs.rearrange("o (q t) k -> q o (t k)", t=PACK)
-            w_raw = []
-            for part in range(2):
-                o_part = slice(part * O // 2, (part + 1) * O // 2)
-                raw = ring.tile([P, O // 2, PACK * K], BF16, name="w_raw", tag="ring", align_bytes=64)
-                nc.sync.dma_start(out=raw[0:HALF, :, :], in_=w_runs[:, o_part, :])
-                nc.sync.dma_start(out=raw[HALF:P, :, 0 : PACK * K - 1], in_=w_runs[:, o_part, 1 : PACK * K])
-                w_raw.append(raw)
-            return w_raw
+        w_runs = coeffs.rearrange("o (q t) k -> q o (t k)", t=PACK)
 
-        def quantise_coeffs(w_raw):
-            w_grouped = ring.tile([P, PASSES, O, PACK], BF16, name="w_grouped", tag="ring", align_bytes=64)
-            for part in range(2):
-                nc.vector.tensor_copy(
-                    out=w_grouped[:, :, part * O // 2 : (part + 1) * O // 2, :],
-                    in_=w_raw[part][:].rearrange("p o (t g h) -> p g o t h", t=PACK, h=2)[:, :, :, :, 0],
-                )
+        def load_coeffs(part):
+            o_part = slice(part * W_PART, (part + 1) * W_PART)
+            raw = basis_pool.tile([P, W_PART, PACK * K], BF16, name="w_raw", tag="basis", align_bytes=64)
+            nc.sync.dma_start(out=raw[0:HALF, :, :], in_=w_runs[:, o_part, :])
+            nc.sync.dma_start(out=raw[HALF:P, :, 0 : PACK * K - 1], in_=w_runs[:, o_part, 1 : PACK * K])
+            return raw
+
+        def regroup_coeffs(part, raw, w_grouped):
+            nc.vector.tensor_copy(
+                out=w_grouped[:, :, part * W_PART : (part + 1) * W_PART, :],
+                in_=raw[:].rearrange("p o (t g h) -> p g o t h", t=PACK, h=2)[:, :, :, :, 0],
+            )
+
+        def quantise_coeffs(w_grouped):
             nc.vector.quantize_mx(
                 out=w_codes[:].rearrange("p g o -> p (g o)").bitcast(FP8X4),
                 scales=w_scales[:].rearrange("p g o -> p (g o)"),
                 in_=w_grouped[:].rearrange("p g o t -> p (g o t)"),
             )
 
-        def tanh_stage(u):
-            for g in range(PASSES):
-                nc.scalar.activation(out=chain[g][:], in_=u, func=ACT.Sigmoid, scale=par[:, g, B3 : B3 + 1], bias=shift[:, 0:1])
+        u_of = {}
+        x_of = {}
+        chain = {}
+        poly = {}
+        basis_of = {}
+        acc_of = {}
+        to_store = []
 
-        def polynomial_start(u):
-            for g in range(PASSES):
-                nc.vector.tensor_scalar(
-                    out=poly[g][:], in0=u, scalar1=coef(g, B8), scalar2=coef(g, B7), op0=ALU.mult, op1=ALU.add
+        def need_u(last_tile):
+            for c in range(len(u_of), last_tile // PASSES + 1):
+                u_of[c] = make_u(x_of[c])
+                if c + 1 < CHUNKS:
+                    x_of[c + 1] = load_x(c + 1)
+
+        def exponentials(tiles):
+            for j in tiles:
+                chain[j] = chain_pool.tile([P, COLS], F32, name="chain", tag="chain", align_bytes=64)
+                nc.scalar.activation(
+                    out=chain[j][:],
+                    in_=u_of[j // PASSES],
+                    func=ACT.Sigmoid,
+                    scale=par[:, j % PASSES, B3 : B3 + 1],
+                    bias=minus_shift[:, 0:1],
                 )
 
-        def polynomial_times_u(u):
-            for g in range(PASSES):
-                nc.vector.tensor_tensor(out=poly[g][:], in0=poly[g][:], in1=u, op=ALU.mult)
+        def logs_of_expm1(tiles):
+            for j in tiles:
+                nc.scalar.activation(
+                    out=chain[j][:], in_=chain[j][:], func=ACT.Ln, scale=math.exp(SHIFT), bias=minus_ones[:, 0:1]
+                )
 
-        def polynomial_step(u, g, j):
+        def sigmoids(tiles):
+            for j in tiles:
+                nc.scalar.activation(
+                    out=chain[j][:], in_=chain[j][:], func=ACT.Sigmoid, scale=neg[:, j % PASSES, B4 : B4 + 1]
+                )
+
+        def outer_logs(tiles):
+            for j in tiles:
+                nc.scalar.activation(out=chain[j][:], in_=chain[j][:], func=ACT.Ln)
+            for j in tiles:
+                nc.scalar.activation(
+                    out=chain[j][:],
+                    in_=chain[j][:],
+                    func=ACT.Ln,
+                    scale=neg[:, j % PASSES, B2 : B2 + 1],
+                    bias=ones[:, 0:1],
+                )
+
+        def polynomials(tiles):
+            for j in tiles:
+                poly[j] = poly_pool.tile([P, COLS], F32, name="poly", tag="poly", align_bytes=64)
+                g = j % PASSES
+                nc.vector.tensor_scalar(
+                    out=poly[j][:],
+                    in0=u_of[j // PASSES],
+                    scalar1=par[:, g, B8 : B8 + 1],
+                    scalar2=par[:, g, B7 : B7 + 1],
+                    op0=ALU.mult,
+                    op1=ALU.add,
+                )
+            for j in tiles:
+                nc.vector.tensor_tensor(out=poly[j][:], in0=poly[j][:], in1=u_of[j // PASSES], op=ALU.mult)
+            for b in (B6, B5):
+                for j in tiles:
+                    nc.vector.scalar_tensor_tensor(
+                        out=poly[j][:],
+                        in0=poly[j][:],
+                        scalar=par[:, j % PASSES, b : b + 1],
+                        in1=u_of[j // PASSES],
+                        op0=ALU.add,
+                        op1=ALU.mult,
+                    )
+
+        def finish(j):
+            basis_of[j] = basis_pool.tile([P, COLS], BF16, name="basis", tag="basis", align_bytes=64)
             nc.vector.scalar_tensor_tensor(
-                out=poly[g][:], in0=poly[g][:], scalar=coef(g, j), in1=u, op0=ALU.add, op1=ALU.mult
+                out=basis_of[j][:],
+                in0=chain[j][:],
+                scalar=par[:, j % PASSES, B1 : B1 + 1],
+                in1=poly[j][:],
+                op0=ALU.mult,
+                op1=ALU.add,
             )
 
-        def log_expm1_stage(u):
-            for g in range(PASSES):
-                nc.scalar.activation(out=chain[g][:], in_=chain[g][:], func=ACT.Ln, scale=math.exp(SHIFT), bias=minus_ones[:, 0:1])
-                polynomial_step(u, g, B6)
-
-        def log1p_pow_stage():
-            for g in range(PASSES):
-                nc.scalar.activation(out=chain[g][:], in_=chain[g][:], func=ACT.Sigmoid, scale=neg[:, g, B4 : B4 + 1])
-            for g in range(PASSES):
-                nc.scalar.activation(out=chain[g][:], in_=chain[g][:], func=ACT.Ln)
-
-        def last_log():
-            for g in range(PASSES):
-                nc.scalar.activation(
-                    out=chain[g][:], in_=chain[g][:], func=ACT.Ln, scale=neg[:, g, B2 : B2 + 1], bias=ones[:, 0:1]
-                )
-
-        def quantise_basis():
-            waiting = []
-            for g in range(PASSES + 1):
-                if g < PASSES:
-                    basis = basis_pool.tile([P, COLS], BF16, name="basis", align_bytes=64)
-                    nc.vector.scalar_tensor_tensor(
-                        out=basis[:], in0=chain[g][:], scalar=coef(g, B1), in1=poly[g][:], op0=ALU.mult, op1=ALU.add
-                    )
-                    waiting.append(basis)
-                if g > 0:
-                    nc.vector.quantize_mx(
-                        out=codes[:, g - 1, :].bitcast(FP8X4), scales=scales[:, g - 1, :], in_=waiting[g - 1][:]
-                    )
-
-        def multiply():
-            acc = psum_acc.tile([P, SUB, O], F32, name="acc")
+        def quantise_and_multiply(j):
+            c, g = divmod(j, PASSES)
+            codes = codes_pool.tile([P, CHUNK], U32, name="codes", align_bytes=64)
+            scales = codes_pool.tile([P, CHUNK], U8, name="scales", align_bytes=64)
+            nc.vector.quantize_mx(out=codes[:].bitcast(FP8X4), scales=scales[:], in_=basis_of[j][:])
+            if g == 0:
+                acc_of[c] = []
+                for s in range(SUB):
+                    acc_s = psum_acc.tile([P, BANK], F32, name="acc", tag="acc%d" % s)
+                    acc_of[c].append(acc_s)
             for s in range(SUB):
                 rows = slice(s * P, (s + 1) * P)
-                for g in range(PASSES):
-                    nc.tensor.matmul_mx(
-                        out=acc[:, s, :],
-                        lhsT=codes[:, g, rows].bitcast(FP8X4),
-                        lhsT_scale=scales[:, g, rows],
-                        rhs=w_codes[:, g, :].bitcast(FP8X4),
-                        rhs_scale=w_scales[:, g, :],
-                        start=(g == 0),
-                        stop=(g == PASSES - 1),
-                    )
-            return acc
+                nc.tensor.matmul_mx(
+                    out=acc_of[c][s][:, 0:O],
+                    lhsT=codes[:, rows].bitcast(FP8X4),
+                    lhsT_scale=scales[:, rows],
+                    rhs=w_codes[:, g, :].bitcast(FP8X4),
+                    rhs_scale=w_scales[:, g, :],
+                    start=(g == 0),
+                    stop=(g == PASSES - 1),
+                )
+            if g == PASSES - 1:
+                to_store.append(c)
 
-        def store(c, acc):
-            res = res_pool.tile([P, SUB, O], F32, name="res")
-            nc.vector.tensor_copy(out=res[:], in_=acc[:])
-            nc.sync.dma_start(out=out_rows[c], in_=res[:])
+        def store():
+            for c in to_store:
+                res = res_pool.tile([P, SUB, O], F32, name="res")
+                for s in range(SUB):
+                    nc.vector.tensor_copy(out=res[:, s, :], in_=acc_of[c][s][:, 0:O])
+                nc.sync.dma_start(out=out_rows[c], in_=res[:])
+            to_store.clear()
 
-        x_next = load_x(0)
+        def finish_batch(tiles):
+            for j in tiles:
+                finish(j)
+                store()
+                if j > tiles[0]:
+                    quantise_and_multiply(j - 1)
+            quantise_and_multiply(tiles[-1])
+
+        x_of[0] = load_x(0)
         make_identity(nc, ident[:])
         i_on_partitions = "(q t) -> q t"
         for h in range(2):
@@ -198,7 +249,7 @@ def tile_photonicbasisactivationlayerintervalaffi_kernel(tc, x, coeffs, b_coef, 
         nc.scalar.dma_start(out=b_all[:], in_=b_coef.rearrange("k j -> (k j)").partition_broadcast(P))
         nc.vector.memset(ones[:], 1.0)
         nc.vector.memset(minus_ones[:], -1.0)
-        nc.vector.memset(shift[:], -SHIFT)
+        nc.vector.memset(minus_shift[:], -SHIFT)
         nc.vector.tensor_copy(out=affine[:, 0, :], in_=alpha_bf[:])
         nc.vector.tensor_copy(out=affine[:, 1, :], in_=beta_bf[:])
         for h in range(2):
@@ -208,30 +259,35 @@ def tile_photonicbasisactivationlayerintervalaffi_kernel(tc, x, coeffs, b_coef, 
                 in_=b_all[half, :].rearrange("p (g h j) -> p g h j", h=2, j=8)[:, :, h, :],
             )
         nc.vector.tensor_scalar(out=neg[:], in0=par[:], scalar1=-1.0, scalar2=None, op0=ALU.mult)
-        nc.vector.tensor_scalar(out=halved[:], in0=par[:], scalar1=0.5, scalar2=None, op0=ALU.mult)
-        u_next = make_u(x_next)
-        x_next = load_x(1)
-        w_raw = load_coeffs()
 
-        acc = None
-        for c in range(CHUNKS):
-            u = u_next
-            tanh_stage(u)
-            polynomial_start(u)
-            if c == 0:
-                quantise_coeffs(w_raw)
-            polynomial_times_u(u)
-            log_expm1_stage(u)
-            log1p_pow_stage()
-            for g in range(PASSES):
-                polynomial_step(u, g, B5)
-            if c > 0:
-                store(c - 1, acc)
-            if c + 1 < CHUNKS:
-                u_next = make_u(x_next)
-            if c + 2 < CHUNKS:
-                x_next = load_x(c + 2)
-            last_log()
-            quantise_basis()
-            acc = multiply()
-        store(CHUNKS - 1, acc)
+        batches = [range(j, min(j + BATCH, TILES)) for j in range(0, TILES, BATCH)]
+        batches.extend([range(0), range(0)])
+        need_u(batches[0][-1])
+        w_raw = [load_coeffs(0), load_coeffs(1)]
+        exponentials(batches[0])
+        logs_of_expm1(batches[0])
+        started = 0
+        for n in range(len(batches) - 2):
+            ready = min(batches[n][0] + AHEAD, TILES)
+            need_u(max(ready, batches[n + 1].stop) - 1)
+            sigmoids(batches[n])
+            exponentials(batches[n + 1])
+            if n == 0:
+                polynomials(range(3))
+                started = 3
+                w_grouped = u_pool.tile([P, PASSES, O, PACK], BF16, name="w_grouped", tag="u", align_bytes=64)
+                for part in range(2):
+                    regroup_coeffs(part, w_raw[part], w_grouped)
+                    w_raw.append(load_coeffs(part + 2))
+            polynomials(range(started, ready))
+            started = ready
+            if n == 0:
+                for part in range(2, W_PARTS):
+                    regroup_coeffs(part, w_raw[part], w_grouped)
+                quantise_coeffs(w_grouped)
+            if batches[n + 2]:
+                need_u(batches[n + 2][-1])
+            outer_logs(batches[n])
+            logs_of_expm1(batches[n + 1])
+            finish_batch(batches[n])
+        store()

@@ -23,8 +23,10 @@ CHUNKS = B // CHUNK
 COLS = CHUNK * PACK
 TILES = CHUNKS * PASSES
 BANK = 512
-BATCH = 7
+BATCH_SIZES = (7, 8)
 AHEAD = 9
+WHOLE = (slice(0, COLS),)
+HALVES = (slice(0, COLS // 2), slice(COLS // 2, COLS))
 W_PARTS = 4
 W_PART = O // W_PARTS
 SHIFT = 32.0
@@ -42,11 +44,11 @@ def tile_photonicbasisactivationlayerintervalaffi_kernel(tc, x, coeffs, b_coef, 
         keep = ctx.enter_context(tc.tile_pool(name="keep", bufs=1))
         x_pool = ctx.enter_context(tc.tile_pool(name="x_pool", bufs=1))
         u_pool = ctx.enter_context(tc.tile_pool(name="u_pool", bufs=3))
-        chain_pool = ctx.enter_context(tc.tile_pool(name="chain_pool", bufs=2 * BATCH))
+        chain_pool = ctx.enter_context(tc.tile_pool(name="chain_pool", bufs=sum(BATCH_SIZES)))
         poly_pool = ctx.enter_context(tc.tile_pool(name="poly_pool", bufs=AHEAD))
         basis_pool = ctx.enter_context(tc.tile_pool(name="basis_pool", bufs=2))
         codes_pool = ctx.enter_context(tc.tile_pool(name="codes_pool", bufs=2))
-        res_pool = ctx.enter_context(tc.tile_pool(name="res_pool", bufs=1))
+        res_pool = ctx.enter_context(tc.tile_pool(name="res_pool", bufs=2))
         psum_x = ctx.enter_context(tc.psum_pool(name="psum_x", bufs=2))
         psum_acc = ctx.enter_context(tc.psum_pool(name="psum_acc", bufs=1))
         ctx.enter_context(tc.manual_schedule())
@@ -59,37 +61,63 @@ def tile_photonicbasisactivationlayerintervalaffi_kernel(tc, x, coeffs, b_coef, 
         beta_bf = keep.tile([P, PACK], BF16, name="beta_bf")
         affine = keep.tile([P, 2, PACK], F32, name="affine")
         ones = keep.tile([P, 1], F32, name="ones")
+        warm = keep.tile([P, 1], F32, name="warm")
         minus_ones = keep.tile([P, 1], F32, name="minus_ones")
         minus_shift = keep.tile([P, 1], F32, name="minus_shift")
         w_codes = keep.tile([P, PASSES, O], U32, name="w_codes", align_bytes=64)
         w_scales = keep.tile([P, PASSES, O], U8, name="w_scales", align_bytes=64)
 
-        def load_x(c):
-            x_twice = x_pool.tile([P, SUB, 2 * I], BF16, name="x_twice")
+        def load_first_x():
+            x_twice = basis_pool.tile([P, SUB, 2 * I], BF16, name="x_twice", tag="basis", align_bytes=64)
             for h in range(2):
-                nc.sync.dma_start(out=x_twice[:, :, h * I : (h + 1) * I], in_=x_rows[c])
+                nc.sync.dma_start(out=x_twice[:, :, h * I : (h + 1) * I], in_=x_rows[0])
             return x_twice
 
-        def make_u(x_twice):
+        def make_first_u(x_twice):
             u = u_pool.tile([P, SUB, P, PACK], F32, name="u", tag="u", align_bytes=64)
-            for pair in range(SUB // 2):
-                x_t = psum_x.tile([P, 2, PACK, P], BF16, name="x_t")
-                for s in range(2):
-                    columns = x_twice[:, 2 * pair + s, :].rearrange("p (m t) -> p t m", t=PACK)
+            for piece in range(2):
+                x_t = psum_x.tile([P, SUB // 2, PACK, P], BF16, name="x_t")
+                for r in range(SUB // 2):
+                    columns = x_twice[:, SUB // 2 * piece + r, :].rearrange("p (m t) -> p t m", t=PACK)
                     for t in range(PACK):
-                        nc.tensor.transpose(x_t[:, s, t, :], columns[:, t, :], ident[:])
-                nc.vector.tensor_tensor(
-                    out=u[:, 2 * pair : 2 * pair + 2, :, :],
-                    in0=x_t[:].rearrange("p s t b -> p s b t"),
-                    in1=affine[:, 0:1, :].unsqueeze(1).to_broadcast([P, 2, P, PACK]),
-                    op=ALU.mult,
-                )
+                        nc.tensor.transpose(x_t[:, r, t, :], columns[:, t, :], ident[:])
+                affine_map(u[:, SUB // 2 * piece : SUB // 2 * (piece + 1), :, :], x_t)
+            return u[:].rearrange("p s b t -> p (s b t)")
+
+        def affine_map(u, x_t):
             nc.vector.tensor_tensor(
-                out=u[:],
-                in0=u[:],
-                in1=affine[:, 1:2, :].unsqueeze(1).to_broadcast([P, SUB, P, PACK]),
+                out=u,
+                in0=x_t[:].rearrange("p r t b -> p r b t"),
+                in1=affine[:, 0:1, :].unsqueeze(1).to_broadcast([P, SUB // 2, P, PACK]),
+                op=ALU.mult,
+            )
+            nc.vector.tensor_tensor(
+                out=u,
+                in0=u,
+                in1=affine[:, 1:2, :].unsqueeze(1).to_broadcast([P, SUB // 2, P, PACK]),
                 op=ALU.add,
             )
+
+        def load_x(c):
+            x_tile = x_pool.tile([P, SUB, I], BF16, name="x_tile")
+            nc.sync.dma_start(out=x_tile[:], in_=x_rows[c])
+            return x_tile
+
+        def make_u(x_tile):
+            x_t = psum_x.tile([P, SUB // 2, PACK, P], BF16, name="x_t")
+            for r in range(SUB // 2):
+                columns = x_tile[:, 2 * r : 2 * r + 2, :].rearrange("p s (q t) -> p t (s q)", t=PACK)
+                for t in range(PACK):
+                    nc.tensor.transpose(x_t[:, r, t, :], columns[:, t, :], ident[:])
+            u_once = basis_pool.tile([P, SUB // 2, P, PACK], F32, name="u_once", tag="basis", align_bytes=64)
+            affine_map(u_once[:], x_t)
+            u = u_pool.tile([P, SUB, P, PACK], F32, name="u", tag="u", align_bytes=64)
+            for odd in range(2):
+                for h in range(2):
+                    nc.sync.dma_start(
+                        out=u[h * HALF : (h + 1) * HALF, odd:SUB:2, :, :],
+                        in_=u_once[odd * HALF : (odd + 1) * HALF, :, :, :],
+                    )
             return u[:].rearrange("p s b t -> p (s b t)")
 
         w_runs = coeffs.rearrange("o (q t) k -> q o (t k)", t=PACK)
@@ -119,25 +147,27 @@ def tile_photonicbasisactivationlayerintervalaffi_kernel(tc, x, coeffs, b_coef, 
         chain = {}
         poly = {}
         basis_of = {}
+        quantised = {}
         acc_of = {}
         to_store = []
 
         def need_u(last_tile):
             for c in range(len(u_of), last_tile // PASSES + 1):
-                u_of[c] = make_u(x_of[c])
+                u_of[c] = make_first_u(x_of[c]) if c == 0 else make_u(x_of[c])
                 if c + 1 < CHUNKS:
                     x_of[c + 1] = load_x(c + 1)
 
         def exponentials(tiles):
             for j in tiles:
                 chain[j] = chain_pool.tile([P, COLS], F32, name="chain", tag="chain", align_bytes=64)
-                nc.scalar.activation(
-                    out=chain[j][:],
-                    in_=u_of[j // PASSES],
-                    func=ACT.Sigmoid,
-                    scale=par[:, j % PASSES, B3 : B3 + 1],
-                    bias=minus_shift[:, 0:1],
-                )
+                for piece in HALVES if j == 0 else WHOLE:
+                    nc.scalar.activation(
+                        out=chain[j][:, piece],
+                        in_=u_of[j // PASSES][:, piece],
+                        func=ACT.Sigmoid,
+                        scale=par[:, j % PASSES, B3 : B3 + 1],
+                        bias=minus_shift[:, 0:1],
+                    )
 
         def logs_of_expm1(tiles):
             for j in tiles:
@@ -155,13 +185,14 @@ def tile_photonicbasisactivationlayerintervalaffi_kernel(tc, x, coeffs, b_coef, 
             for j in tiles:
                 nc.scalar.activation(out=chain[j][:], in_=chain[j][:], func=ACT.Ln)
             for j in tiles:
-                nc.scalar.activation(
-                    out=chain[j][:],
-                    in_=chain[j][:],
-                    func=ACT.Ln,
-                    scale=neg[:, j % PASSES, B2 : B2 + 1],
-                    bias=ones[:, 0:1],
-                )
+                for piece in last_pieces(j):
+                    nc.scalar.activation(
+                        out=chain[j][:, piece],
+                        in_=chain[j][:, piece],
+                        func=ACT.Ln,
+                        scale=neg[:, j % PASSES, B2 : B2 + 1],
+                        bias=ones[:, 0:1],
+                    )
 
         def polynomials(tiles):
             for j in tiles:
@@ -188,31 +219,38 @@ def tile_photonicbasisactivationlayerintervalaffi_kernel(tc, x, coeffs, b_coef, 
                         op1=ALU.mult,
                     )
 
-        def finish(j):
-            basis_of[j] = basis_pool.tile([P, COLS], BF16, name="basis", tag="basis", align_bytes=64)
+        def last_pieces(j):
+            return HALVES if j == TILES - 1 else WHOLE
+
+        def finish(j, piece):
+            if piece.start == 0:
+                basis_of[j] = basis_pool.tile([P, COLS], BF16, name="basis", tag="basis", align_bytes=64)
             nc.vector.scalar_tensor_tensor(
-                out=basis_of[j][:],
-                in0=chain[j][:],
+                out=basis_of[j][:, piece],
+                in0=chain[j][:, piece],
                 scalar=par[:, j % PASSES, B1 : B1 + 1],
-                in1=poly[j][:],
+                in1=poly[j][:, piece],
                 op0=ALU.mult,
                 op1=ALU.add,
             )
 
-        def quantise_and_multiply(j):
+        def quantise_and_multiply(j, piece):
             c, g = divmod(j, PASSES)
-            codes = codes_pool.tile([P, CHUNK], U32, name="codes", align_bytes=64)
-            scales = codes_pool.tile([P, CHUNK], U8, name="scales", align_bytes=64)
-            nc.vector.quantize_mx(out=codes[:].bitcast(FP8X4), scales=scales[:], in_=basis_of[j][:])
-            if g == 0:
-                acc_of[c] = []
-                for s in range(SUB):
-                    acc_s = psum_acc.tile([P, BANK], F32, name="acc", tag="acc%d" % s)
-                    acc_of[c].append(acc_s)
-            for s in range(SUB):
+            if piece.start == 0:
+                codes = codes_pool.tile([P, CHUNK], U32, name="codes", align_bytes=64)
+                scales = codes_pool.tile([P, CHUNK], U8, name="scales", align_bytes=64)
+                quantised[j] = (codes, scales)
+            codes, scales = quantised[j]
+            words = slice(piece.start // PACK, piece.stop // PACK)
+            nc.vector.quantize_mx(
+                out=codes[:, words].bitcast(FP8X4), scales=scales[:, words], in_=basis_of[j][:, piece]
+            )
+            for s in range(words.start // P, words.stop // P):
                 rows = slice(s * P, (s + 1) * P)
+                if g == 0:
+                    acc_of[s] = psum_acc.tile([P, BANK], F32, name="acc", tag="acc%d" % s)
                 nc.tensor.matmul_mx(
-                    out=acc_of[c][s][:, 0:O],
+                    out=acc_of[s][:, 0:O],
                     lhsT=codes[:, rows].bitcast(FP8X4),
                     lhsT_scale=scales[:, rows],
                     rhs=w_codes[:, g, :].bitcast(FP8X4),
@@ -220,34 +258,35 @@ def tile_photonicbasisactivationlayerintervalaffi_kernel(tc, x, coeffs, b_coef, 
                     start=(g == 0),
                     stop=(g == PASSES - 1),
                 )
-            if g == PASSES - 1:
-                to_store.append(c)
+                if g == PASSES - 1:
+                    to_store.append((c, s))
 
         def store():
-            for c in to_store:
-                res = res_pool.tile([P, SUB, O], F32, name="res")
-                for s in range(SUB):
-                    nc.vector.tensor_copy(out=res[:, s, :], in_=acc_of[c][s][:, 0:O])
-                nc.sync.dma_start(out=out_rows[c], in_=res[:])
+            for c, s in to_store:
+                res = res_pool.tile([P, O], F32, name="res")
+                nc.vector.tensor_copy(out=res[:], in_=acc_of[s][:, 0:O])
+                nc.sync.dma_start(out=out_rows[c][:, s, :], in_=res[:])
             to_store.clear()
 
         def finish_batch(tiles):
-            for j in tiles:
-                finish(j)
+            pieces = [(j, piece) for j in tiles for piece in last_pieces(j)]
+            for m in range(len(pieces)):
+                finish(*pieces[m])
                 store()
-                if j > tiles[0]:
-                    quantise_and_multiply(j - 1)
-            quantise_and_multiply(tiles[-1])
+                if m > 0:
+                    quantise_and_multiply(*pieces[m - 1])
+            quantise_and_multiply(*pieces[-1])
 
-        x_of[0] = load_x(0)
+        x_of[0] = load_first_x()
+        nc.vector.memset(ones[:], 1.0)
         make_identity(nc, ident[:])
+        nc.scalar.dma_start(out=b_all[:], in_=b_coef.rearrange("k j -> (k j)").partition_broadcast(P))
         i_on_partitions = "(q t) -> q t"
         for h in range(2):
             half = slice(h * HALF, (h + 1) * HALF)
             nc.scalar.dma_start(out=alpha_bf[half, :], in_=alpha.rearrange(i_on_partitions, t=PACK))
             nc.scalar.dma_start(out=beta_bf[half, :], in_=beta.rearrange(i_on_partitions, t=PACK))
-        nc.scalar.dma_start(out=b_all[:], in_=b_coef.rearrange("k j -> (k j)").partition_broadcast(P))
-        nc.vector.memset(ones[:], 1.0)
+        nc.scalar.activation(out=warm[:], in_=ones[:], func=ACT.Sigmoid)
         nc.vector.memset(minus_ones[:], -1.0)
         nc.vector.memset(minus_shift[:], -SHIFT)
         nc.vector.tensor_copy(out=affine[:, 0, :], in_=alpha_bf[:])
@@ -260,9 +299,12 @@ def tile_photonicbasisactivationlayerintervalaffi_kernel(tc, x, coeffs, b_coef, 
             )
         nc.vector.tensor_scalar(out=neg[:], in0=par[:], scalar1=-1.0, scalar2=None, op0=ALU.mult)
 
-        batches = [range(j, min(j + BATCH, TILES)) for j in range(0, TILES, BATCH)]
+        batches = []
+        while not batches or batches[-1].stop < TILES:
+            begin = batches[-1].stop if batches else 0
+            batches.append(range(begin, min(begin + BATCH_SIZES[len(batches) % 2], TILES)))
         batches.extend([range(0), range(0)])
-        need_u(batches[0][-1])
+        need_u(batches[1][-1])
         w_raw = [load_coeffs(0), load_coeffs(1)]
         exponentials(batches[0])
         logs_of_expm1(batches[0])

@@ -24,7 +24,7 @@ COLS = CHUNK * PACK
 TILES = CHUNKS * PASSES
 BANK = 512
 BATCH_SIZES = (7, 8)
-AHEAD = 9
+AHEAD = 8
 WHOLE = (slice(0, COLS),)
 HALVES = (slice(0, COLS // 2), slice(COLS // 2, COLS))
 W_PARTS = 4
@@ -43,12 +43,13 @@ def tile_photonicbasisactivationlayerintervalaffi_kernel(tc, x, coeffs, b_coef, 
     with ExitStack() as ctx:
         keep = ctx.enter_context(tc.tile_pool(name="keep", bufs=1))
         x_pool = ctx.enter_context(tc.tile_pool(name="x_pool", bufs=1))
+        once_pool = ctx.enter_context(tc.tile_pool(name="once_pool", bufs=1))
         u_pool = ctx.enter_context(tc.tile_pool(name="u_pool", bufs=3))
         chain_pool = ctx.enter_context(tc.tile_pool(name="chain_pool", bufs=sum(BATCH_SIZES)))
         poly_pool = ctx.enter_context(tc.tile_pool(name="poly_pool", bufs=AHEAD))
         basis_pool = ctx.enter_context(tc.tile_pool(name="basis_pool", bufs=2))
         codes_pool = ctx.enter_context(tc.tile_pool(name="codes_pool", bufs=2))
-        res_pool = ctx.enter_context(tc.tile_pool(name="res_pool", bufs=2))
+        res_pool = ctx.enter_context(tc.tile_pool(name="res_pool", bufs=1))
         psum_x = ctx.enter_context(tc.psum_pool(name="psum_x", bufs=2))
         psum_acc = ctx.enter_context(tc.psum_pool(name="psum_acc", bufs=1))
         ctx.enter_context(tc.manual_schedule())
@@ -109,7 +110,7 @@ def tile_photonicbasisactivationlayerintervalaffi_kernel(tc, x, coeffs, b_coef, 
                 columns = x_tile[:, 2 * r : 2 * r + 2, :].rearrange("p s (q t) -> p t (s q)", t=PACK)
                 for t in range(PACK):
                     nc.tensor.transpose(x_t[:, r, t, :], columns[:, t, :], ident[:])
-            u_once = basis_pool.tile([P, SUB // 2, P, PACK], F32, name="u_once", tag="basis", align_bytes=64)
+            u_once = once_pool.tile([P, SUB // 2, P, PACK], F32, name="u_once")
             affine_map(u_once[:], x_t)
             u = u_pool.tile([P, SUB, P, PACK], F32, name="u", tag="u", align_bytes=64)
             for odd in range(2):
@@ -149,6 +150,7 @@ def tile_photonicbasisactivationlayerintervalaffi_kernel(tc, x, coeffs, b_coef, 
         basis_of = {}
         quantised = {}
         acc_of = {}
+        res_of = {}
         to_store = []
 
         def need_u(last_tile):
@@ -182,42 +184,50 @@ def tile_photonicbasisactivationlayerintervalaffi_kernel(tc, x, coeffs, b_coef, 
                 )
 
         def outer_logs(tiles):
-            for j in tiles:
-                nc.scalar.activation(out=chain[j][:], in_=chain[j][:], func=ACT.Ln)
-            for j in tiles:
-                for piece in last_pieces(j):
-                    nc.scalar.activation(
-                        out=chain[j][:, piece],
-                        in_=chain[j][:, piece],
-                        func=ACT.Ln,
-                        scale=neg[:, j % PASSES, B2 : B2 + 1],
-                        bias=ones[:, 0:1],
-                    )
+            for j in range(tiles[0], tiles[-1] + 2):
+                if j <= tiles[-1]:
+                    nc.scalar.activation(out=chain[j][:], in_=chain[j][:], func=ACT.Ln)
+                if j > tiles[0]:
+                    for piece in last_pieces(j - 1):
+                        nc.scalar.activation(
+                            out=chain[j - 1][:, piece],
+                            in_=chain[j - 1][:, piece],
+                            func=ACT.Ln,
+                            scale=neg[:, (j - 1) % PASSES, B2 : B2 + 1],
+                            bias=ones[:, 0:1],
+                        )
 
-        def polynomials(tiles):
-            for j in tiles:
+        horner = [(j, step) for a in range(0, TILES, 2) for step in range(4) for j in (a, a + 1)]
+        position = {"horner": 0}
+
+        def horner_step(j, step):
+            g = j % PASSES
+            need_u(j)
+            u = u_of[j // PASSES]
+            if step == 0:
                 poly[j] = poly_pool.tile([P, COLS], F32, name="poly", tag="poly", align_bytes=64)
-                g = j % PASSES
                 nc.vector.tensor_scalar(
                     out=poly[j][:],
-                    in0=u_of[j // PASSES],
+                    in0=u,
                     scalar1=par[:, g, B8 : B8 + 1],
                     scalar2=par[:, g, B7 : B7 + 1],
                     op0=ALU.mult,
                     op1=ALU.add,
                 )
-            for j in tiles:
-                nc.vector.tensor_tensor(out=poly[j][:], in0=poly[j][:], in1=u_of[j // PASSES], op=ALU.mult)
-            for b in (B6, B5):
-                for j in tiles:
-                    nc.vector.scalar_tensor_tensor(
-                        out=poly[j][:],
-                        in0=poly[j][:],
-                        scalar=par[:, j % PASSES, b : b + 1],
-                        in1=u_of[j // PASSES],
-                        op0=ALU.add,
-                        op1=ALU.mult,
-                    )
+            elif step == 1:
+                nc.vector.tensor_tensor(out=poly[j][:], in0=poly[j][:], in1=u, op=ALU.mult)
+            else:
+                b = B6 if step == 2 else B5
+                nc.vector.scalar_tensor_tensor(
+                    out=poly[j][:], in0=poly[j][:], scalar=par[:, g, b : b + 1], in1=u, op0=ALU.add, op1=ALU.mult
+                )
+
+        def polynomials(steps, finished):
+            for j, step in horner[position["horner"] : position["horner"] + steps]:
+                if j >= finished + AHEAD:
+                    break
+                horner_step(j, step)
+                position["horner"] += 1
 
         def last_pieces(j):
             return HALVES if j == TILES - 1 else WHOLE
@@ -262,10 +272,15 @@ def tile_photonicbasisactivationlayerintervalaffi_kernel(tc, x, coeffs, b_coef, 
                     to_store.append((c, s))
 
         def store():
-            for c, s in to_store:
-                res = res_pool.tile([P, O], F32, name="res")
-                nc.vector.tensor_copy(out=res[:], in_=acc_of[s][:, 0:O])
-                nc.sync.dma_start(out=out_rows[c][:, s, :], in_=res[:])
+            if not to_store:
+                return
+            c = to_store[0][0]
+            groups = slice(to_store[0][1], to_store[-1][1] + 1)
+            if groups.start == 0:
+                res_of[c] = res_pool.tile([P, SUB, O], F32, name="res")
+            for s in range(groups.start, groups.stop):
+                nc.vector.tensor_copy(out=res_of[c][:, s, :], in_=acc_of[s][:, 0:O])
+            nc.sync.dma_start(out=out_rows[c][:, groups, :], in_=res_of[c][:, groups, :])
             to_store.clear()
 
         def finish_batch(tiles):
@@ -275,7 +290,10 @@ def tile_photonicbasisactivationlayerintervalaffi_kernel(tc, x, coeffs, b_coef, 
                 store()
                 if m > 0:
                     quantise_and_multiply(*pieces[m - 1])
+                polynomials(2, pieces[m][0] + 1)
             quantise_and_multiply(*pieces[-1])
+            if tiles[-1] == TILES - 1:
+                store()
 
         x_of[0] = load_first_x()
         nc.vector.memset(ones[:], 1.0)
@@ -308,28 +326,25 @@ def tile_photonicbasisactivationlayerintervalaffi_kernel(tc, x, coeffs, b_coef, 
         w_raw = [load_coeffs(0), load_coeffs(1)]
         exponentials(batches[0])
         logs_of_expm1(batches[0])
-        started = 0
         for n in range(len(batches) - 2):
-            ready = min(batches[n][0] + AHEAD, TILES)
-            need_u(max(ready, batches[n + 1].stop) - 1)
+            need_u(batches[n + 1].stop - 1)
             sigmoids(batches[n])
             exponentials(batches[n + 1])
             if n == 0:
-                polynomials(range(3))
-                started = 3
-                w_grouped = u_pool.tile([P, PASSES, O, PACK], BF16, name="w_grouped", tag="u", align_bytes=64)
+                w_grouped = poly_pool.tile([P, PASSES, O, PACK], BF16, name="w_grouped", tag="poly", align_bytes=64)
+                polynomials(16, 0)
                 for part in range(2):
                     regroup_coeffs(part, w_raw[part], w_grouped)
                     w_raw.append(load_coeffs(part + 2))
-            polynomials(range(started, ready))
-            started = ready
-            if n == 0:
+                polynomials(8, 0)
                 for part in range(2, W_PARTS):
                     regroup_coeffs(part, w_raw[part], w_grouped)
                 quantise_coeffs(w_grouped)
+            else:
+                polynomials(12, batches[n][0])
             if batches[n + 2]:
                 need_u(batches[n + 2][-1])
+            polynomials(4 * AHEAD, batches[n][0])
             outer_logs(batches[n])
             logs_of_expm1(batches[n + 1])
             finish_batch(batches[n])
-        store()

@@ -23,11 +23,13 @@ CHUNKS = B // CHUNK
 COLS = CHUNK * PACK
 TILES = CHUNKS * PASSES
 BANK = 512
-BATCH_SIZES = (7, 8)
+BATCH = 8
+QUAD = 4
+PAIR = 2
 AHEAD = 8
 WHOLE = (slice(0, COLS),)
 HALVES = (slice(0, COLS // 2), slice(COLS // 2, COLS))
-W_PARTS = 4
+W_PARTS = 2
 W_PART = O // W_PARTS
 SHIFT = 32.0
 B1, B2, B3, B4, B5, B6, B7, B8 = range(8)
@@ -43,12 +45,11 @@ def tile_photonicbasisactivationlayerintervalaffi_kernel(tc, x, coeffs, b_coef, 
     with ExitStack() as ctx:
         keep = ctx.enter_context(tc.tile_pool(name="keep", bufs=1))
         x_pool = ctx.enter_context(tc.tile_pool(name="x_pool", bufs=1))
-        once_pool = ctx.enter_context(tc.tile_pool(name="once_pool", bufs=1))
         u_pool = ctx.enter_context(tc.tile_pool(name="u_pool", bufs=3))
-        chain_pool = ctx.enter_context(tc.tile_pool(name="chain_pool", bufs=sum(BATCH_SIZES)))
+        chain_pool = ctx.enter_context(tc.tile_pool(name="chain_pool", bufs=2 * BATCH // QUAD))
         poly_pool = ctx.enter_context(tc.tile_pool(name="poly_pool", bufs=AHEAD))
-        basis_pool = ctx.enter_context(tc.tile_pool(name="basis_pool", bufs=2))
-        codes_pool = ctx.enter_context(tc.tile_pool(name="codes_pool", bufs=2))
+        basis_pool = ctx.enter_context(tc.tile_pool(name="basis_pool", bufs=1))
+        codes_pool = ctx.enter_context(tc.tile_pool(name="codes_pool", bufs=1))
         res_pool = ctx.enter_context(tc.tile_pool(name="res_pool", bufs=1))
         psum_x = ctx.enter_context(tc.psum_pool(name="psum_x", bufs=2))
         psum_acc = ctx.enter_context(tc.psum_pool(name="psum_acc", bufs=1))
@@ -110,7 +111,7 @@ def tile_photonicbasisactivationlayerintervalaffi_kernel(tc, x, coeffs, b_coef, 
                 columns = x_tile[:, 2 * r : 2 * r + 2, :].rearrange("p s (q t) -> p t (s q)", t=PACK)
                 for t in range(PACK):
                     nc.tensor.transpose(x_t[:, r, t, :], columns[:, t, :], ident[:])
-            u_once = once_pool.tile([P, SUB // 2, P, PACK], F32, name="u_once")
+            u_once = basis_pool.tile([P, SUB // 2, P, PACK], F32, name="u_once", tag="basis", align_bytes=64)
             affine_map(u_once[:], x_t)
             u = u_pool.tile([P, SUB, P, PACK], F32, name="u", tag="u", align_bytes=64)
             for odd in range(2):
@@ -145,13 +146,17 @@ def tile_photonicbasisactivationlayerintervalaffi_kernel(tc, x, coeffs, b_coef, 
 
         u_of = {}
         x_of = {}
-        chain = {}
+        quad_of = {}
         poly = {}
         basis_of = {}
         quantised = {}
         acc_of = {}
         res_of = {}
         to_store = []
+
+        def chain(j, piece=WHOLE[0]):
+            begin = j % QUAD * COLS
+            return quad_of[j // QUAD][:, begin + piece.start : begin + piece.stop]
 
         def need_u(last_tile):
             for c in range(len(u_of), last_tile // PASSES + 1):
@@ -161,10 +166,11 @@ def tile_photonicbasisactivationlayerintervalaffi_kernel(tc, x, coeffs, b_coef, 
 
         def exponentials(tiles):
             for j in tiles:
-                chain[j] = chain_pool.tile([P, COLS], F32, name="chain", tag="chain", align_bytes=64)
+                if j % QUAD == 0:
+                    quad_of[j // QUAD] = chain_pool.tile([P, QUAD * COLS], F32, name="chain", align_bytes=64)
                 for piece in HALVES if j == 0 else WHOLE:
                     nc.scalar.activation(
-                        out=chain[j][:, piece],
+                        out=chain(j, piece),
                         in_=u_of[j // PASSES][:, piece],
                         func=ACT.Sigmoid,
                         scale=par[:, j % PASSES, B3 : B3 + 1],
@@ -172,26 +178,27 @@ def tile_photonicbasisactivationlayerintervalaffi_kernel(tc, x, coeffs, b_coef, 
                     )
 
         def logs_of_expm1(tiles):
-            for j in tiles:
+            for j in tiles[::QUAD]:
+                quad = quad_of[j // QUAD]
                 nc.scalar.activation(
-                    out=chain[j][:], in_=chain[j][:], func=ACT.Ln, scale=math.exp(SHIFT), bias=minus_ones[:, 0:1]
+                    out=quad[:], in_=quad[:], func=ACT.Ln, scale=math.exp(SHIFT), bias=minus_ones[:, 0:1]
                 )
 
         def sigmoids(tiles):
             for j in tiles:
                 nc.scalar.activation(
-                    out=chain[j][:], in_=chain[j][:], func=ACT.Sigmoid, scale=neg[:, j % PASSES, B4 : B4 + 1]
+                    out=chain(j), in_=chain(j), func=ACT.Sigmoid, scale=neg[:, j % PASSES, B4 : B4 + 1]
                 )
 
         def outer_logs(tiles):
             for j in range(tiles[0], tiles[-1] + 2):
                 if j <= tiles[-1]:
-                    nc.scalar.activation(out=chain[j][:], in_=chain[j][:], func=ACT.Ln)
+                    nc.scalar.activation(out=chain(j), in_=chain(j), func=ACT.Ln)
                 if j > tiles[0]:
                     for piece in last_pieces(j - 1):
                         nc.scalar.activation(
-                            out=chain[j - 1][:, piece],
-                            in_=chain[j - 1][:, piece],
+                            out=chain(j - 1, piece),
+                            in_=chain(j - 1, piece),
                             func=ACT.Ln,
                             scale=neg[:, (j - 1) % PASSES, B2 : B2 + 1],
                             bias=ones[:, 0:1],
@@ -233,30 +240,34 @@ def tile_photonicbasisactivationlayerintervalaffi_kernel(tc, x, coeffs, b_coef, 
             return HALVES if j == TILES - 1 else WHOLE
 
         def finish(j, piece):
-            if piece.start == 0:
-                basis_of[j] = basis_pool.tile([P, COLS], BF16, name="basis", tag="basis", align_bytes=64)
+            if j % PAIR == 0:
+                basis_of[j // PAIR] = basis_pool.tile(
+                    [P, PAIR * COLS], BF16, name="basis", tag="basis", align_bytes=64
+                )
+            begin = j % PAIR * COLS
             nc.vector.scalar_tensor_tensor(
-                out=basis_of[j][:, piece],
-                in0=chain[j][:, piece],
+                out=basis_of[j // PAIR][:, begin + piece.start : begin + piece.stop],
+                in0=chain(j, piece),
                 scalar=par[:, j % PASSES, B1 : B1 + 1],
                 in1=poly[j][:, piece],
                 op0=ALU.mult,
                 op1=ALU.add,
             )
 
-        def quantise_and_multiply(j, piece):
-            c, g = divmod(j, PASSES)
-            if piece.start == 0:
-                codes = codes_pool.tile([P, CHUNK], U32, name="codes", align_bytes=64)
-                scales = codes_pool.tile([P, CHUNK], U8, name="scales", align_bytes=64)
-                quantised[j] = (codes, scales)
-            codes, scales = quantised[j]
-            words = slice(piece.start // PACK, piece.stop // PACK)
+        def quantise_and_multiply(pair, begin, end):
+            if begin == 0:
+                codes = codes_pool.tile([P, PAIR * CHUNK], U32, name="codes", align_bytes=64)
+                scales = codes_pool.tile([P, PAIR * CHUNK], U8, name="scales", align_bytes=64)
+                quantised[pair] = (codes, scales)
+            codes, scales = quantised[pair]
+            words = slice(begin // PACK, end // PACK)
             nc.vector.quantize_mx(
-                out=codes[:, words].bitcast(FP8X4), scales=scales[:, words], in_=basis_of[j][:, piece]
+                out=codes[:, words].bitcast(FP8X4), scales=scales[:, words], in_=basis_of[pair][:, begin:end]
             )
-            for s in range(words.start // P, words.stop // P):
-                rows = slice(s * P, (s + 1) * P)
+            for group in range(words.start // P, words.stop // P):
+                c, g = divmod(pair * PAIR + group // SUB, PASSES)
+                s = group % SUB
+                rows = slice(group * P, (group + 1) * P)
                 if g == 0:
                     acc_of[s] = psum_acc.tile([P, BANK], F32, name="acc", tag="acc%d" % s)
                 nc.tensor.matmul_mx(
@@ -284,15 +295,19 @@ def tile_photonicbasisactivationlayerintervalaffi_kernel(tc, x, coeffs, b_coef, 
             to_store.clear()
 
         def finish_batch(tiles):
-            pieces = [(j, piece) for j in tiles for piece in last_pieces(j)]
-            for m in range(len(pieces)):
-                finish(*pieces[m])
+            for j in tiles[: -1 if tiles[-1] == TILES - 1 else len(tiles)]:
+                finish(j, WHOLE[0])
                 store()
-                if m > 0:
-                    quantise_and_multiply(*pieces[m - 1])
-                polynomials(2, pieces[m][0] + 1)
-            quantise_and_multiply(*pieces[-1])
+                polynomials(2, j + 1)
+                if j % PAIR == PAIR - 1:
+                    quantise_and_multiply(j // PAIR, 0, PAIR * COLS)
             if tiles[-1] == TILES - 1:
+                pair = TILES // PAIR - 1
+                finish(TILES - 1, HALVES[0])
+                quantise_and_multiply(pair, 0, COLS)
+                finish(TILES - 1, HALVES[1])
+                quantise_and_multiply(pair, COLS, COLS + COLS // 2)
+                quantise_and_multiply(pair, COLS + COLS // 2, PAIR * COLS)
                 store()
 
         x_of[0] = load_first_x()
@@ -317,13 +332,10 @@ def tile_photonicbasisactivationlayerintervalaffi_kernel(tc, x, coeffs, b_coef, 
             )
         nc.vector.tensor_scalar(out=neg[:], in0=par[:], scalar1=-1.0, scalar2=None, op0=ALU.mult)
 
-        batches = []
-        while not batches or batches[-1].stop < TILES:
-            begin = batches[-1].stop if batches else 0
-            batches.append(range(begin, min(begin + BATCH_SIZES[len(batches) % 2], TILES)))
+        batches = [range(j, j + BATCH) for j in range(0, TILES, BATCH)]
         batches.extend([range(0), range(0)])
         need_u(batches[1][-1])
-        w_raw = [load_coeffs(0), load_coeffs(1)]
+        w_raw = load_coeffs(0)
         exponentials(batches[0])
         logs_of_expm1(batches[0])
         for n in range(len(batches) - 2):
@@ -332,16 +344,14 @@ def tile_photonicbasisactivationlayerintervalaffi_kernel(tc, x, coeffs, b_coef, 
             exponentials(batches[n + 1])
             if n == 0:
                 w_grouped = poly_pool.tile([P, PASSES, O, PACK], BF16, name="w_grouped", tag="poly", align_bytes=64)
-                polynomials(16, 0)
-                for part in range(2):
-                    regroup_coeffs(part, w_raw[part], w_grouped)
-                    w_raw.append(load_coeffs(part + 2))
                 polynomials(8, 0)
-                for part in range(2, W_PARTS):
-                    regroup_coeffs(part, w_raw[part], w_grouped)
+                regroup_coeffs(0, w_raw, w_grouped)
+                w_raw = load_coeffs(1)
+                polynomials(16, 0)
+                regroup_coeffs(1, w_raw, w_grouped)
                 quantise_coeffs(w_grouped)
             else:
-                polynomials(12, batches[n][0])
+                polynomials(4, batches[n][0])
             if batches[n + 2]:
                 need_u(batches[n + 2][-1])
             polynomials(4 * AHEAD, batches[n][0])

@@ -27,6 +27,7 @@ BATCH = 8
 QUAD = 4
 PAIR = 2
 AHEAD = 8
+SPARE = 2
 WHOLE = (slice(0, COLS),)
 HALVES = (slice(0, COLS // 2), slice(COLS // 2, COLS))
 W_PARTS = 2
@@ -212,7 +213,10 @@ def tile_photonicbasisactivationlayerintervalaffi_kernel(tc, x, coeffs, b_coef, 
             need_u(j)
             u = u_of[j // PASSES]
             if step == 0:
-                poly[j] = poly_pool.tile([P, COLS], F32, name="poly", tag="poly", align_bytes=64)
+                if TILES - BATCH <= j < TILES - BATCH + SPARE:
+                    poly[j] = u_pool.tile([P, COLS], F32, name="poly", tag="u", align_bytes=64)
+                else:
+                    poly[j] = poly_pool.tile([P, COLS], F32, name="poly", tag="poly", align_bytes=64)
                 nc.vector.tensor_scalar(
                     out=poly[j][:],
                     in0=u,
@@ -231,7 +235,7 @@ def tile_photonicbasisactivationlayerintervalaffi_kernel(tc, x, coeffs, b_coef, 
 
         def polynomials(steps, finished):
             for j, step in horner[position["horner"] : position["horner"] + steps]:
-                if j >= finished + AHEAD:
+                if j >= finished + AHEAD + (SPARE if j >= TILES - BATCH else 0):
                     break
                 horner_step(j, step)
                 position["horner"] += 1
@@ -290,7 +294,10 @@ def tile_photonicbasisactivationlayerintervalaffi_kernel(tc, x, coeffs, b_coef, 
             if groups.start == 0:
                 res_of[c] = res_pool.tile([P, SUB, O], F32, name="res")
             for s in range(groups.start, groups.stop):
-                nc.vector.tensor_copy(out=res_of[c][:, s, :], in_=acc_of[s][:, 0:O])
+                if c == CHUNKS - 1 and s % 2 == 1:
+                    nc.scalar.copy(out=res_of[c][:, s, :], in_=acc_of[s][:, 0:O])
+                else:
+                    nc.vector.tensor_copy(out=res_of[c][:, s, :], in_=acc_of[s][:, 0:O])
             nc.sync.dma_start(out=out_rows[c][:, groups, :], in_=res_of[c][:, groups, :])
             to_store.clear()
 
@@ -354,7 +361,7 @@ def tile_photonicbasisactivationlayerintervalaffi_kernel(tc, x, coeffs, b_coef, 
                 polynomials(4, batches[n][0])
             if batches[n + 2]:
                 need_u(batches[n + 2][-1])
-            polynomials(4 * AHEAD, batches[n][0])
+            polynomials(4 * (AHEAD + SPARE), batches[n][0])
             outer_logs(batches[n])
             logs_of_expm1(batches[n + 1])
             finish_batch(batches[n])

import math
from contextlib import ExitStack

import concourse.mybir as mybir
from concourse.masks import make_identity

F32 = mybir.dt.float32
BF16 = mybir.dt.bfloat16
U32 = mybir.dt.uint32
U8 = mybir.dt.uint8
FP8X4 = mybir.dt.float8_e4m3fn_x4
ACT = mybir.ActivationFunctionType
ALU = mybir.AluOpType

B, I, O, K = 4096, 256, 128, 16
P = 128
PACK = 4
HALF = P // 2
PASSES = K // 2
SUB = 4
CHUNK = SUB * P
CHUNKS = B // CHUNK
COLS = CHUNK * PACK
TILES = CHUNKS * PASSES
BANK = 512
BATCH = 8
QUAD = 4
PAIR = 2
AHEAD = 8
SPARE = 2
WHOLE = (slice(0, COLS),)
HALVES = (slice(0, COLS // 2), slice(COLS // 2, COLS))
W_PARTS = 2
W_PART = O // W_PARTS
SHIFT = 32.0
B1, B2, B3, B4, B5, B6, B7, B8 = range(8)

FLOPS = 2 * B * I * K * O


def tile_photonicbasisactivationlayerintervalaffi_kernel(tc, x, coeffs, b_coef, alpha, beta, out):
    nc = tc.nc
    x_rows = x.rearrange("(c p s) i -> c p s i", p=P, s=SUB)
    out_rows = out.rearrange("(c p s) o -> c p s o", p=P, s=SUB)

    with ExitStack() as ctx:
        keep = ctx.enter_context(tc.tile_pool(name="keep", bufs=1))
        x_pool = ctx.enter_context(tc.tile_pool(name="x_pool", bufs=1))
        u_pool = ctx.enter_context(tc.tile_pool(name="u_pool", bufs=3))
        chain_pool = ctx.enter_context(tc.tile_pool(name="chain_pool", bufs=2 * BATCH // QUAD))
        poly_pool = ctx.enter_context(tc.tile_pool(name="poly_pool", bufs=AHEAD))
        basis_pool = ctx.enter_context(tc.tile_pool(name="basis_pool", bufs=1))
        codes_pool = ctx.enter_context(tc.tile_pool(name="codes_pool", bufs=1))
        res_pool = ctx.enter_context(tc.tile_pool(name="res_pool", bufs=1))
        psum_x = ctx.enter_context(tc.psum_pool(name="psum_x", bufs=2))
        psum_acc = ctx.enter_context(tc.psum_pool(name="psum_acc", bufs=1))
        ctx.enter_context(tc.manual_schedule())

        ident = keep.tile([P, P], BF16, name="ident")
        b_all = keep.tile([P, K * 8], BF16, name="b_all")
        par = keep.tile([P, PASSES, 8], F32, name="par")
        neg = keep.tile([P, PASSES, 8], F32, name="neg")
        alpha_bf = keep.tile([P, PACK], BF16, name="alpha_bf")
        beta_bf = keep.tile([P, PACK], BF16, name="beta_bf")
        affine = keep.tile([P, 2, PACK], F32, name="affine")
        ones = keep.tile([P, 1], F32, name="ones")
        warm = keep.tile([P, 1], F32, name="warm")
        minus_ones = keep.tile([P, 1], F32, name="minus_ones")
        minus_shift = keep.tile([P, 1], F32, name="minus_shift")
        w_codes = keep.tile([P, PASSES, O], U32, name="w_codes", align_bytes=64)
        w_scales = keep.tile([P, PASSES, O], U8, name="w_scales", align_bytes=64)

        def load_first_x():
            x_twice = basis_pool.tile([P, SUB, 2 * I], BF16, name="x_twice", tag="basis", align_bytes=64)
            for h in range(2):
                nc.sync.dma_start(out=x_twice[:, :, h * I : (h + 1) * I], in_=x_rows[0])
            return x_twice

        def make_first_u(x_twice):
            u = u_pool.tile([P, SUB, P, PACK], F32, name="u", tag="u", align_bytes=64)
            for piece in range(2):
                x_t = psum_x.tile([P, SUB // 2, PACK, P], BF16, name="x_t")
                for r in range(SUB // 2):
                    columns = x_twice[:, SUB // 2 * piece + r, :].rearrange("p (m t) -> p t m", t=PACK)
                    for t in range(PACK):
                        nc.tensor.transpose(x_t[:, r, t, :], columns[:, t, :], ident[:])
                affine_map(u[:, SUB // 2 * piece : SUB // 2 * (piece + 1), :, :], x_t)
            return u[:].rearrange("p s b t -> p (s b t)")

        def affine_map(u, x_t):
            nc.vector.tensor_tensor(
                out=u,
                in0=x_t[:].rearrange("p r t b -> p r b t"),
                in1=affine[:, 0:1, :].unsqueeze(1).to_broadcast([P, SUB // 2, P, PACK]),
                op=ALU.mult,
            )
            nc.vector.tensor_tensor(
                out=u,
                in0=u,
                in1=affine[:, 1:2, :].unsqueeze(1).to_broadcast([P, SUB // 2, P, PACK]),
                op=ALU.add,
            )

        def load_x(c):
            x_tile = x_pool.tile([P, SUB, I], BF16, name="x_tile")
            nc.sync.dma_start(out=x_tile[:], in_=x_rows[c])
            return x_tile

        def make_u(x_tile):
            x_t = psum_x.tile([P, SUB // 2, PACK, P], BF16, name="x_t")
            for r in range(SUB // 2):
                columns = x_tile[:, 2 * r : 2 * r + 2, :].rearrange("p s (q t) -> p t (s q)", t=PACK)
                for t in range(PACK):
                    nc.tensor.transpose(x_t[:, r, t, :], columns[:, t, :], ident[:])
            u_once = basis_pool.tile([P, SUB // 2, P, PACK], F32, name="u_once", tag="basis", align_bytes=64)
            affine_map(u_once[:], x_t)
            u = u_pool.tile([P, SUB, P, PACK], F32, name="u", tag="u", align_bytes=64)
            for odd in range(2):
                for h in range(2):
                    nc.sync.dma_start(
                        out=u[h * HALF : (h + 1) * HALF, odd:SUB:2, :, :],
                        in_=u_once[odd * HALF : (odd + 1) * HALF, :, :, :],
                    )
            return u[:].rearrange("p s b t -> p (s b t)")

        w_runs = coeffs.rearrange("o (q t) k -> q o (t k)", t=PACK)

        def load_coeffs(part):
            o_part = slice(part * W_PART, (part + 1) * W_PART)
            raw = basis_pool.tile([P, W_PART, PACK * K], BF16, name="w_raw", tag="basis", align_bytes=64)
            nc.sync.dma_start(out=raw[0:HALF, :, :], in_=w_runs[:, o_part, :])
            nc.sync.dma_start(out=raw[HALF:P, :, 0 : PACK * K - 1], in_=w_runs[:, o_part, 1 : PACK * K])
            return raw

        def regroup_coeffs(part, raw, w_grouped):
            nc.vector.tensor_copy(
                out=w_grouped[:, :, part * W_PART : (part + 1) * W_PART, :],
                in_=raw[:].rearrange("p o (t g h) -> p g o t h", t=PACK, h=2)[:, :, :, :, 0],
            )

        def quantise_coeffs(w_grouped):
            nc.vector.quantize_mx(
                out=w_codes[:].rearrange("p g o -> p (g o)").bitcast(FP8X4),
                scales=w_scales[:].rearrange("p g o -> p (g o)"),
                in_=w_grouped[:].rearrange("p g o t -> p (g o t)"),
            )

        u_of = {}
        x_of = {}
        quad_of = {}
        poly = {}
        basis_of = {}
        quantised = {}
        acc_of = {}
        res_of = {}
        to_store = []

        def chain(j, piece=WHOLE[0]):
            begin = j % QUAD * COLS
            return quad_of[j // QUAD][:, begin + piece.start : begin + piece.stop]

        def need_u(last_tile):
            for c in range(len(u_of), last_tile // PASSES + 1):
                u_of[c] = make_first_u(x_of[c]) if c == 0 else make_u(x_of[c])
                if c + 1 < CHUNKS:
                    x_of[c + 1] = load_x(c + 1)

        def exponentials(tiles):
            for j in tiles:
                if j % QUAD == 0:
                    quad_of[j // QUAD] = chain_pool.tile([P, QUAD * COLS], F32, name="chain", align_bytes=64)
                for piece in HALVES if j == 0 else WHOLE:
                    nc.scalar.activation(
                        out=chain(j, piece),
                        in_=u_of[j // PASSES][:, piece],
                        func=ACT.Sigmoid,
                        scale=par[:, j % PASSES, B3 : B3 + 1],
                        bias=minus_shift[:, 0:1],
                    )

        def logs_of_expm1(tiles):
            for j in tiles[::QUAD]:
                quad = quad_of[j // QUAD]
                nc.scalar.activation(
                    out=quad[:], in_=quad[:], func=ACT.Ln, scale=math.exp(SHIFT), bias=minus_ones[:, 0:1]
                )

        def sigmoids(tiles):
            for j in tiles:
                nc.scalar.activation(
                    out=chain(j), in_=chain(j), func=ACT.Sigmoid, scale=neg[:, j % PASSES, B4 : B4 + 1]
                )

        def outer_logs(tiles):
            for j in range(tiles[0], tiles[-1] + 2):
                if j <= tiles[-1]:
                    nc.scalar.activation(out=chain(j), in_=chain(j), func=ACT.Ln)
                if j > tiles[0]:
                    for piece in last_pieces(j - 1):
                        nc.scalar.activation(
                            out=chain(j - 1, piece),
                            in_=chain(j - 1, piece),
                            func=ACT.Ln,
                            scale=neg[:, (j - 1) % PASSES, B2 : B2 + 1],
                            bias=ones[:, 0:1],
                        )

        horner = [(j, step) for a in range(0, TILES, 2) for step in range(4) for j in (a, a + 1)]
        position = {"horner": 0}

        def horner_step(j, step):
            g = j % PASSES
            need_u(j)
            u = u_of[j // PASSES]
            if step == 0:
                if TILES - BATCH <= j < TILES - BATCH + SPARE:
                    poly[j] = u_pool.tile([P, COLS], F32, name="poly", tag="u", align_bytes=64)
                else:
                    poly[j] = poly_pool.tile([P, COLS], F32, name="poly", tag="poly", align_bytes=64)
                nc.vector.tensor_scalar(
                    out=poly[j][:],
                    in0=u,
                    scalar1=par[:, g, B8 : B8 + 1],
                    scalar2=par[:, g, B7 : B7 + 1],
                    op0=ALU.mult,
                    op1=ALU.add,
                )
            elif step == 1:
                nc.vector.tensor_tensor(out=poly[j][:], in0=poly[j][:], in1=u, op=ALU.mult)
            else:
                b = B6 if step == 2 else B5
                nc.vector.scalar_tensor_tensor(
                    out=poly[j][:], in0=poly[j][:], scalar=par[:, g, b : b + 1], in1=u, op0=ALU.add, op1=ALU.mult
                )

        def polynomials(steps, finished):
            for j, step in horner[position["horner"] : position["horner"] + steps]:
                if j >= finished + AHEAD + (SPARE if j >= TILES - BATCH else 0):
                    break
                horner_step(j, step)
                position["horner"] += 1

        def last_pieces(j):
            return HALVES if j == TILES - 1 else WHOLE

        def finish(j, piece):
            if j % PAIR == 0:
                basis_of[j // PAIR] = basis_pool.tile(
                    [P, PAIR * COLS], BF16, name="basis", tag="basis", align_bytes=64
                )
            begin = j % PAIR * COLS
            nc.vector.scalar_tensor_tensor(
                out=basis_of[j // PAIR][:, begin + piece.start : begin + piece.stop],
                in0=chain(j, piece),
                scalar=par[:, j % PASSES, B1 : B1 + 1],
                in1=poly[j][:, piece],
                op0=ALU.mult,
                op1=ALU.add,
            )

        def quantise_and_multiply(pair, begin, end):
            if begin == 0:
                codes = codes_pool.tile([P, PAIR * CHUNK], U32, name="codes", align_bytes=64)
                scales = codes_pool.tile([P, PAIR * CHUNK], U8, name="scales", align_bytes=64)
                quantised[pair] = (codes, scales)
            codes, scales = quantised[pair]
            words = slice(begin // PACK, end // PACK)
            nc.vector.quantize_mx(
                out=codes[:, words].bitcast(FP8X4), scales=scales[:, words], in_=basis_of[pair][:, begin:end]
            )
            for group in range(words.start // P, words.stop // P):
                c, g = divmod(pair * PAIR + group // SUB, PASSES)
                s = group % SUB
                rows = slice(group * P, (group + 1) * P)
                if g == 0:
                    acc_of[s] = psum_acc.tile([P, BANK], F32, name="acc", tag="acc%d" % s)
                nc.tensor.matmul_mx(
                    out=acc_of[s][:, 0:O],
                    lhsT=codes[:, rows].bitcast(FP8X4),
                    lhsT_scale=scales[:, rows],
                    rhs=w_codes[:, g, :].bitcast(FP8X4),
                    rhs_scale=w_scales[:, g, :],
                    start=(g == 0),
                    stop=(g == PASSES - 1),
                )
                if g == PASSES - 1:
                    to_store.append((c, s))

        def store():
            if not to_store:
                return
            c = to_store[0][0]
            groups = slice(to_store[0][1], to_store[-1][1] + 1)
            if groups.start == 0:
                res_of[c] = res_pool.tile([P, SUB, O], F32, name="res")
            for s in range(groups.start, groups.stop):
                if c == CHUNKS - 1 and s % 2 == 1:
                    nc.scalar.copy(out=res_of[c][:, s, :], in_=acc_of[s][:, 0:O])
                else:
                    nc.vector.tensor_copy(out=res_of[c][:, s, :], in_=acc_of[s][:, 0:O])
            nc.sync.dma_start(out=out_rows[c][:, groups, :], in_=res_of[c][:, groups, :])
            to_store.clear()

        def finish_batch(tiles):
            for j in tiles[: -1 if tiles[-1] == TILES - 1 else len(tiles)]:
                finish(j, WHOLE[0])
                store()
                polynomials(2, j + 1)
                if j % PAIR == PAIR - 1:
                    quantise_and_multiply(j // PAIR, 0, PAIR * COLS)
            if tiles[-1] == TILES - 1:
                pair = TILES // PAIR - 1
                finish(TILES - 1, HALVES[0])
                quantise_and_multiply(pair, 0, COLS)
                finish(TILES - 1, HALVES[1])
                quantise_and_multiply(pair, COLS, COLS + COLS // 2)
                quantise_and_multiply(pair, COLS + COLS // 2, PAIR * COLS)
                store()

        x_of[0] = load_first_x()
        nc.vector.memset(ones[:], 1.0)
        make_identity(nc, ident[:])
        nc.scalar.dma_start(out=b_all[:], in_=b_coef.rearrange("k j -> (k j)").partition_broadcast(P))
        i_on_partitions = "(q t) -> q t"
        for h in range(2):
            half = slice(h * HALF, (h + 1) * HALF)
            nc.scalar.dma_start(out=alpha_bf[half, :], in_=alpha.rearrange(i_on_partitions, t=PACK))
            nc.scalar.dma_start(out=beta_bf[half, :], in_=beta.rearrange(i_on_partitions, t=PACK))
        nc.scalar.activation(out=warm[:], in_=ones[:], func=ACT.Sigmoid)
        nc.vector.memset(minus_ones[:], -1.0)
        nc.vector.memset(minus_shift[:], -SHIFT)
        nc.vector.tensor_copy(out=affine[:, 0, :], in_=alpha_bf[:])
        nc.vector.tensor_copy(out=affine[:, 1, :], in_=beta_bf[:])
        for h in range(2):
            half = slice(h * HALF, (h + 1) * HALF)
            nc.vector.tensor_copy(
                out=par[half, :, :],
                in_=b_all[half, :].rearrange("p (g h j) -> p g h j", h=2, j=8)[:, :, h, :],
            )
        nc.vector.tensor_scalar(out=neg[:], in0=par[:], scalar1=-1.0, scalar2=None, op0=ALU.mult)

        batches = [range(j, j + BATCH) for j in range(0, TILES, BATCH)]
        batches.extend([range(0), range(0)])
        need_u(batches[1][-1])
        w_raw = load_coeffs(0)
        exponentials(batches[0])
        logs_of_expm1(batches[0])
        for n in range(len(batches) - 2):
            need_u(batches[n + 1].stop - 1)
            sigmoids(batches[n])
            exponentials(batches[n + 1])
            if n == 0:
                w_grouped = poly_pool.tile([P, PASSES, O, PACK], BF16, name="w_grouped", tag="poly", align_bytes=64)
                polynomials(8, 0)
                regroup_coeffs(0, w_raw, w_grouped)
                w_raw = load_coeffs(1)
                polynomials(16, 0)
                regroup_coeffs(1, w_raw, w_grouped)
                quantise_coeffs(w_grouped)
            else:
                polynomials(4, batches[n][0])
            if batches[n + 2]:
                need_u(batches[n + 2][-1])
            polynomials(4 * (AHEAD + SPARE), batches[n][0])
            outer_logs(batches[n])
            logs_of_expm1(batches[n + 1])
            finish_batch(batches[n])
